import numpy as np
import ml_dtypes

BF16 = ml_dtypes.bfloat16


def bf(x):
    return np.asarray(x, np.float32).astype(BF16)


def f32(x):
    return np.asarray(x, np.float32)


def f64(x):
    return np.asarray(x).astype(np.float64)


def striped(idx):
    return np.tile(idx.reshape(-1, 16).T, (8, 1))


S, D, M, N = 2048, 128, 128, 256


def sigmoid(v):
    return 1.0 / (1.0 + np.exp(-v))


def setup_inputs():
    return {"table": bf(0.1 * np.random.standard_normal((S, D))), "pos": bf(0.5 * np.random.standard_normal((D, N))), "w": bf(np.random.standard_normal((D, M)) / np.sqrt(D)), "b": f32(0.1 * np.random.standard_normal((M, 1))), "offs": striped(np.random.permutation(np.tile(np.arange(S), 2))[:N])}


def reference(table, pos, w, b, offs):
    idx = offs[:16].T.reshape(-1)
    word_part = f64(w).T @ f64(table)[idx].T
    pos_part = f64(w).T @ f64(pos)
    return sigmoid(np.sqrt(D) * word_part + pos_part + f64(b))

@@ -1,0 +1,66 @@
+import math
+
+import concourse.mybir as mybir
+from concourse.masks import make_identity
+
+BF16, F32, U16 = mybir.dt.bfloat16, mybir.dt.float32, mybir.dt.uint16
+MULT, ADD = mybir.AluOpType.mult, mybir.AluOpType.add
+SIGMOID = mybir.ActivationFunctionType.Sigmoid
+
+WORDS, FEATURES, SCORES, TOKENS = 2048, 128, 128, 256
+P = 128
+BLOCKS = 4
+GROUPS = WORDS // (BLOCKS * P)
+FLOPS = 2 * 2 * FEATURES * SCORES * TOKENS
+
+
+def tile_resonetictransformer_kernel(tc, table, pos, w, b, offs, out):
+    nc = tc.nc
+    with (
+        tc.tile_pool(name="held", bufs=1) as held,
+        tc.psum_pool(name="psum", bufs=1) as psum,
+    ):
+        table_groups = table.rearrange("(g t p) k -> g p t k", t=BLOCKS, p=P)
+        rows = [held.tile([P, BLOCKS, FEATURES], BF16, name=f"rows{g}") for g in range(GROUPS)]
+        for g in range(GROUPS):
+            queue = nc.sync if g % 2 == 0 else nc.scalar
+            queue.dma_start(rows[g][:], table_groups[g])
+
+        offsets = held.tile([P, TOKENS // 16], U16, name="offsets")
+        nc.sync.dma_start(offsets[:], offs)
+        weights = held.tile([FEATURES, SCORES], BF16, name="weights")
+        nc.sync.dma_start(weights[:], w)
+        positions = held.tile([FEATURES, TOKENS], BF16, name="positions")
+        nc.scalar.dma_start(positions[:], pos)
+        bias = held.tile([SCORES, 1], F32, name="bias")
+        nc.sync.dma_start(bias[:], b)
+
+        identity = held.tile([P, P], BF16, name="identity")
+        make_identity(nc, identity[:])
+
+        words = held.tile([FEATURES, WORDS], BF16, name="words")
+        for g in range(GROUPS):
+            flipped = psum.tile([FEATURES, BLOCKS * P], BF16, name=f"flipped{g}")
+            for t in range(BLOCKS):
+                nc.tensor.transpose(flipped[:, t * P : (t + 1) * P], rows[g][:, t, :], identity[:])
+            group_of_words = words[:, g * BLOCKS * P : (g + 1) * BLOCKS * P]
+            if g % 2 == 0:
+                nc.vector.tensor_copy(group_of_words, flipped[:])
+            else:
+                nc.scalar.copy(group_of_words, flipped[:])
+
+        pos_product = psum.tile([SCORES, TOKENS], F32, name="pos_product")
+        nc.tensor.matmul(pos_product[:], weights[:], positions[:], start=True, stop=True)
+        pos_and_bias = held.tile([SCORES, TOKENS], F32, name="pos_and_bias")
+        nc.vector.tensor_scalar(pos_and_bias[:], pos_product[:], bias[:], None, ADD)
+
+        word_product = psum.tile([SCORES, TOKENS], F32, name="word_product")
+        nc.tensor.matmul(word_product[:], weights[:], words[:].indirect(offsets[:]), start=True, stop=True)
+
+        logits = held.tile([SCORES, TOKENS], F32, name="logits")
+        nc.vector.scalar_tensor_tensor(
+            logits[:], word_product[:], math.sqrt(FEATURES), pos_and_bias[:], MULT, ADD
+        )
+        scores = held.tile([SCORES, TOKENS], F32, name="scores")
+        nc.scalar.activation(scores[:], logits[:], SIGMOID)
+        nc.sync.dma_start(out, scores[:])

@@ -43,11 +43,7 @@ def tile_resonetictransformer_kernel(tc, table, pos, w, b, offs, out):
             flipped = psum.tile([FEATURES, BLOCKS * P], BF16, name=f"flipped{g}")
             for t in range(BLOCKS):
                 nc.tensor.transpose(flipped[:, t * P : (t + 1) * P], rows[g][:, t, :], identity[:])
-            group_of_words = words[:, g * BLOCKS * P : (g + 1) * BLOCKS * P]
-            if g % 2 == 0:
-                nc.vector.tensor_copy(group_of_words, flipped[:])
-            else:
-                nc.scalar.copy(group_of_words, flipped[:])
+            nc.vector.tensor_copy(words[:, g * BLOCKS * P : (g + 1) * BLOCKS * P], flipped[:])
 
         pos_product = psum.tile([SCORES, TOKENS], F32, name="pos_product")
         nc.tensor.matmul(pos_product[:], weights[:], positions[:], start=True, stop=True)

@@ -4,10 +4,11 @@ import concourse.mybir as mybir
 from concourse.masks import make_identity
 
 BF16, F32, U16 = mybir.dt.bfloat16, mybir.dt.float32, mybir.dt.uint16
-MULT, ADD = mybir.AluOpType.mult, mybir.AluOpType.add
+MULT = mybir.AluOpType.mult
 SIGMOID = mybir.ActivationFunctionType.Sigmoid
 
 WORDS, FEATURES, SCORES, TOKENS = 2048, 128, 128, 256
+WORD_SCALE = math.sqrt(FEATURES)
 P = 128
 BLOCKS = 4
 GROUPS = WORDS // (BLOCKS * P)
@@ -20,6 +21,11 @@ def tile_resonetictransformer_kernel(tc, table, pos, w, b, offs, out):
         tc.tile_pool(name="held", bufs=1) as held,
         tc.psum_pool(name="psum", bufs=1) as psum,
     ):
+        weights = held.tile([FEATURES, SCORES], BF16, name="weights")
+        nc.sync.dma_start(weights[:], w)
+        positions = held.tile([FEATURES, TOKENS], BF16, name="positions")
+        nc.scalar.dma_start(positions[:], pos)
+
         table_groups = table.rearrange("(g t p) k -> g p t k", t=BLOCKS, p=P)
         rows = [held.tile([P, BLOCKS, FEATURES], BF16, name=f"rows{g}") for g in range(GROUPS)]
         for g in range(GROUPS):
@@ -28,15 +34,18 @@ def tile_resonetictransformer_kernel(tc, table, pos, w, b, offs, out):
 
         offsets = held.tile([P, TOKENS // 16], U16, name="offsets")
         nc.sync.dma_start(offsets[:], offs)
-        weights = held.tile([FEATURES, SCORES], BF16, name="weights")
-        nc.sync.dma_start(weights[:], w)
-        positions = held.tile([FEATURES, TOKENS], BF16, name="positions")
-        nc.scalar.dma_start(positions[:], pos)
         bias = held.tile([SCORES, 1], F32, name="bias")
         nc.sync.dma_start(bias[:], b)
 
         identity = held.tile([P, P], BF16, name="identity")
         make_identity(nc, identity[:])
+
+        weights_f32 = held.tile([FEATURES, SCORES], F32, name="weights_f32")
+        nc.vector.tensor_copy(weights_f32[:], weights[:])
+        positions_f32 = held.tile([FEATURES, TOKENS], F32, name="positions_f32")
+        nc.vector.tensor_scalar(positions_f32[:], positions[:], 1.0 / WORD_SCALE, None, MULT)
+        products = psum.tile([SCORES, TOKENS], F32, name="products")
+        nc.tensor.matmul(products[:], weights_f32[:], positions_f32[:], start=True, stop=False)
 
         words = held.tile([FEATURES, WORDS], BF16, name="words")
         for g in range(GROUPS):
@@ -45,18 +54,8 @@ def tile_resonetictransformer_kernel(tc, table, pos, w, b, offs, out):
                 nc.tensor.transpose(flipped[:, t * P : (t + 1) * P], rows[g][:, t, :], identity[:])
             nc.vector.tensor_copy(words[:, g * BLOCKS * P : (g + 1) * BLOCKS * P], flipped[:])
 
-        pos_product = psum.tile([SCORES, TOKENS], F32, name="pos_product")
-        nc.tensor.matmul(pos_product[:], weights[:], positions[:], start=True, stop=True)
-        pos_and_bias = held.tile([SCORES, TOKENS], F32, name="pos_and_bias")
-        nc.vector.tensor_scalar(pos_and_bias[:], pos_product[:], bias[:], None, ADD)
+        nc.tensor.matmul(products[:], weights[:], words[:].indirect(offsets[:]), start=False, stop=True)
 
-        word_product = psum.tile([SCORES, TOKENS], F32, name="word_product")
-        nc.tensor.matmul(word_product[:], weights[:], words[:].indirect(offsets[:]), start=True, stop=True)
-
-        logits = held.tile([SCORES, TOKENS], F32, name="logits")
-        nc.vector.scalar_tensor_tensor(
-            logits[:], word_product[:], math.sqrt(FEATURES), pos_and_bias[:], MULT, ADD
-        )
         scores = held.tile([SCORES, TOKENS], F32, name="scores")
-        nc.scalar.activation(scores[:], logits[:], SIGMOID)
+        nc.scalar.activation(scores[:], products[:], SIGMOID, bias=bias[:], scale=WORD_SCALE)
         nc.sync.dma_start(out, scores[:])

@@ -12,6 +12,8 @@ WORD_SCALE = math.sqrt(FEATURES)
 P = 128
 BLOCKS = 4
 GROUPS = WORDS // (BLOCKS * P)
+BANK = 512
+WARMUPS = 4
 FLOPS = 2 * 2 * FEATURES * SCORES * TOKENS
 
 
@@ -25,6 +27,8 @@ def tile_resonetictransformer_kernel(tc, table, pos, w, b, offs, out):
         nc.sync.dma_start(weights[:], w)
         positions = held.tile([FEATURES, TOKENS], BF16, name="positions")
         nc.scalar.dma_start(positions[:], pos)
+        bias = held.tile([SCORES, 1], F32, name="bias")
+        nc.scalar.dma_start(bias[:], b)
 
         table_groups = table.rearrange("(g t p) k -> g p t k", t=BLOCKS, p=P)
         rows = [held.tile([P, BLOCKS, FEATURES], BF16, name=f"rows{g}") for g in range(GROUPS)]
@@ -34,8 +38,12 @@ def tile_resonetictransformer_kernel(tc, table, pos, w, b, offs, out):
 
         offsets = held.tile([P, TOKENS // 16], U16, name="offsets")
         nc.sync.dma_start(offsets[:], offs)
-        bias = held.tile([SCORES, 1], F32, name="bias")
-        nc.sync.dma_start(bias[:], b)
+
+        zeros = held.tile([P, BANK], BF16, name="zeros")
+        nc.gpsimd.memset(zeros[:], 0.0)
+        unread = psum.tile([P, BANK], F32, name="unread")
+        for i in range(WARMUPS):
+            nc.tensor.matmul(unread[:], zeros[:, :P], zeros[:], start=True, stop=True)
 
         identity = held.tile([P, P], BF16, name="identity")
         make_identity(nc, identity[:])

@@ -27,8 +27,6 @@ def tile_resonetictransformer_kernel(tc, table, pos, w, b, offs, out):
         nc.sync.dma_start(weights[:], w)
         positions = held.tile([FEATURES, TOKENS], BF16, name="positions")
         nc.scalar.dma_start(positions[:], pos)
-        bias = held.tile([SCORES, 1], F32, name="bias")
-        nc.scalar.dma_start(bias[:], b)
 
         table_groups = table.rearrange("(g t p) k -> g p t k", t=BLOCKS, p=P)
         rows = [held.tile([P, BLOCKS, FEATURES], BF16, name=f"rows{g}") for g in range(GROUPS)]
@@ -38,15 +36,19 @@ def tile_resonetictransformer_kernel(tc, table, pos, w, b, offs, out):
 
         offsets = held.tile([P, TOKENS // 16], U16, name="offsets")
         nc.sync.dma_start(offsets[:], offs)
-
-        zeros = held.tile([P, BANK], BF16, name="zeros")
-        nc.gpsimd.memset(zeros[:], 0.0)
-        unread = psum.tile([P, BANK], F32, name="unread")
-        for i in range(WARMUPS):
-            nc.tensor.matmul(unread[:], zeros[:, :P], zeros[:], start=True, stop=True)
+        bias = held.tile([SCORES, 1], F32, name="bias")
+        nc.sync.dma_start(bias[:], b)
 
         identity = held.tile([P, P], BF16, name="identity")
         make_identity(nc, identity[:])
+
+        zeros = held.tile([P, BANK], BF16, name="zeros")
+        nc.vector.memset(zeros[:], 0.0)
+        unread_product = psum.tile([P, BANK], F32, name="unread_product")
+        for i in range(WARMUPS):
+            nc.tensor.matmul(unread_product[:], zeros[:, :P], zeros[:], start=True, stop=True)
+        unread_sigmoid = held.tile([P, 1], F32, name="unread_sigmoid")
+        nc.scalar.activation(unread_sigmoid[:], zeros[:, :1], SIGMOID)
 
         weights_f32 = held.tile([FEATURES, SCORES], F32, name="weights_f32")
         nc.vector.tensor_copy(weights_f32[:], weights[:])

@@ -28,7 +28,7 @@ def tile_resonetictransformer_kernel(tc, table, pos, w, b, offs, out):
         positions = held.tile([FEATURES, TOKENS], BF16, name="positions")
         nc.scalar.dma_start(positions[:], pos)
 
-        table_groups = table.rearrange("(g t p) k -> g p t k", t=BLOCKS, p=P)
+        table_groups = table.rearrange("(g p t) k -> g p t k", t=BLOCKS, p=P)
         rows = [held.tile([P, BLOCKS, FEATURES], BF16, name=f"rows{g}") for g in range(GROUPS)]
         for g in range(GROUPS):
             queue = nc.sync if g % 2 == 0 else nc.scalar
@@ -62,7 +62,12 @@ def tile_resonetictransformer_kernel(tc, table, pos, w, b, offs, out):
             flipped = psum.tile([FEATURES, BLOCKS * P], BF16, name=f"flipped{g}")
             for t in range(BLOCKS):
                 nc.tensor.transpose(flipped[:, t * P : (t + 1) * P], rows[g][:, t, :], identity[:])
-            nc.vector.tensor_copy(words[:, g * BLOCKS * P : (g + 1) * BLOCKS * P], flipped[:])
+            in_order = words[:, g * BLOCKS * P : (g + 1) * BLOCKS * P].rearrange("k (p t) -> k p t", t=BLOCKS)
+            by_block = flipped[:].rearrange("k (t p) -> k p t", t=BLOCKS)
+            if g % 2 == 0:
+                nc.vector.tensor_copy(in_order, by_block)
+            else:
+                nc.scalar.copy(in_order, by_block)
 
         nc.tensor.matmul(products[:], weights[:], words[:].indirect(offsets[:]), start=False, stop=True)
 

import math

import concourse.mybir as mybir
from concourse.masks import make_identity

BF16, F32, U16 = mybir.dt.bfloat16, mybir.dt.float32, mybir.dt.uint16
MULT = mybir.AluOpType.mult
SIGMOID = mybir.ActivationFunctionType.Sigmoid

WORDS, FEATURES, SCORES, TOKENS = 2048, 128, 128, 256
WORD_SCALE = math.sqrt(FEATURES)
P = 128
BLOCKS = 4
GROUPS = WORDS // (BLOCKS * P)
BANK = 512
WARMUPS = 4
FLOPS = 2 * 2 * FEATURES * SCORES * TOKENS


def tile_resonetictransformer_kernel(tc, table, pos, w, b, offs, out):
    nc = tc.nc
    with (
        tc.tile_pool(name="held", bufs=1) as held,
        tc.psum_pool(name="psum", bufs=1) as psum,
    ):
        weights = held.tile([FEATURES, SCORES], BF16, name="weights")
        nc.sync.dma_start(weights[:], w)
        positions = held.tile([FEATURES, TOKENS], BF16, name="positions")
        nc.scalar.dma_start(positions[:], pos)

        table_groups = table.rearrange("(g p t) k -> g p t k", t=BLOCKS, p=P)
        rows = [held.tile([P, BLOCKS, FEATURES], BF16, name=f"rows{g}") for g in range(GROUPS)]
        for g in range(GROUPS):
            queue = nc.sync if g % 2 == 0 else nc.scalar
            queue.dma_start(rows[g][:], table_groups[g])

        offsets = held.tile([P, TOKENS // 16], U16, name="offsets")
        nc.sync.dma_start(offsets[:], offs)
        bias = held.tile([SCORES, 1], F32, name="bias")
        nc.sync.dma_start(bias[:], b)

        identity = held.tile([P, P], BF16, name="identity")
        make_identity(nc, identity[:])

        zeros = held.tile([P, BANK], BF16, name="zeros")
        nc.vector.memset(zeros[:], 0.0)
        unread_product = psum.tile([P, BANK], F32, name="unread_product")
        for i in range(WARMUPS):
            nc.tensor.matmul(unread_product[:], zeros[:, :P], zeros[:], start=True, stop=True)
        unread_sigmoid = held.tile([P, 1], F32, name="unread_sigmoid")
        nc.scalar.activation(unread_sigmoid[:], zeros[:, :1], SIGMOID)

        weights_f32 = held.tile([FEATURES, SCORES], F32, name="weights_f32")
        nc.vector.tensor_copy(weights_f32[:], weights[:])
        positions_f32 = held.tile([FEATURES, TOKENS], F32, name="positions_f32")
        nc.vector.tensor_scalar(positions_f32[:], positions[:], 1.0 / WORD_SCALE, None, MULT)
        products = psum.tile([SCORES, TOKENS], F32, name="products")
        nc.tensor.matmul(products[:], weights_f32[:], positions_f32[:], start=True, stop=False)

        words = held.tile([FEATURES, WORDS], BF16, name="words")
        for g in range(GROUPS):
            flipped = psum.tile([FEATURES, BLOCKS * P], BF16, name=f"flipped{g}")
            for t in range(BLOCKS):
                nc.tensor.transpose(flipped[:, t * P : (t + 1) * P], rows[g][:, t, :], identity[:])
            in_order = words[:, g * BLOCKS * P : (g + 1) * BLOCKS * P].rearrange("k (p t) -> k p t", t=BLOCKS)
            by_block = flipped[:].rearrange("k (t p) -> k p t", t=BLOCKS)
            if g % 2 == 0:
                nc.vector.tensor_copy(in_order, by_block)
            else:
                nc.scalar.copy(in_order, by_block)

        nc.tensor.matmul(products[:], weights[:], words[:].indirect(offsets[:]), start=False, stop=True)

        scores = held.tile([SCORES, TOKENS], F32, name="scores")
        nc.scalar.activation(scores[:], products[:], SIGMOID, bias=bias[:], scale=WORD_SCALE)
        nc.sync.dma_start(out, scores[:])
